import numpy as np
import ml_dtypes


def mxq(x, axis, fmt="e4m3"):
    dtype, down = {"e4m3": (ml_dtypes.float8_e4m3fn, 7), "e5m2": (ml_dtypes.float8_e5m2, 14)}[fmt]
    v = np.moveaxis(np.asarray(x, np.float32).astype(ml_dtypes.bfloat16).astype(np.float64), axis, -1)
    blocks = v.reshape(v.shape[:-1] + (-1, 32))
    amax = np.abs(blocks).max(-1, keepdims=True)
    byte = np.maximum(np.where(amax > 0, np.frexp(amax)[1] - 1 + 127, 0) - down, 1)
    scale = np.exp2(byte - 127.0)
    codes = (blocks / scale).astype(np.float32).astype(dtype).astype(np.float64)
    return np.moveaxis((codes * scale).reshape(v.shape), -1, axis)


WIDE = False


def mx_kscale(k):
    if not WIDE:
        return np.ones(k)
    levels = np.array([30, -30])
    if k % 512:
        return np.exp2(np.random.permutation(np.resize(levels, k // 32))).repeat(32)
    a = np.empty((k // 512, 16))
    for p in range(k // 512):
        a[p, :8] = np.random.permutation(np.resize(levels, 8))
        for g in range(8):
            far = levels[np.abs(levels - a[p, g]) >= 10]
            a[p, g + 8] = far[np.random.randint(len(far))]
    return np.exp2(a.ravel()).repeat(32)


BF16 = ml_dtypes.bfloat16


def bf(x):
    return np.asarray(x, np.float32).astype(BF16)


def f64(x):
    return np.asarray(x).astype(np.float64)


N, DIM, DIM_INNER, T, H, W = 2, 1024, 512, 4, 16, 16
L = T * H * W
EPS = 1e-5


def setup_inputs():
    s = mx_kscale(DIM_INNER)
    return {"x": bf(np.random.standard_normal((N, DIM, T, H, W))),
            "attn_out": bf(np.random.standard_normal((N, DIM_INNER, T, H, W)) * 0.25 * s[None, :, None, None, None]),
            "w_out": bf(np.random.standard_normal((DIM, DIM_INNER)) * 3.0 / np.sqrt(DIM_INNER) / s[None, :]),
            "b_out": bf(0.3 + np.random.standard_normal(DIM) * 0.4)}


def reference(x, attn_out, w_out, b_out):
    a = f64(attn_out).reshape(N, DIM_INNER, L)
    p = (mxq(f64(w_out), 1, "e5m2") @ mxq(a, 1, "e4m3")) + f64(b_out)[None, :, None]
    mu = p.mean(axis=(1, -1), keepdims=True)
    var = p.var(axis=(1, -1), keepdims=True)
    p = (p - mu) / np.sqrt(var + EPS)
    return f64(x) + p.reshape(N, DIM, T, H, W)

@@ -1,0 +1,583 @@
+from contextlib import ExitStack
+
+import concourse.mybir as mybir
+from concourse.masks import make_identity
+
+F32 = mybir.dt.float32
+BF16 = mybir.dt.bfloat16
+U32 = mybir.dt.uint32
+U8 = mybir.dt.uint8
+E4M3 = mybir.dt.float8_e4m3fn_x4
+E5M2 = mybir.dt.float8_e5m2_x4
+ALU = mybir.AluOpType
+ACT = mybir.ActivationFunctionType
+
+SAMPLES, DIM, INNER, L = 2, 1024, 512, 1024
+EPS = 1e-5
+FLOPS = 2 * SAMPLES * DIM * INNER * L
+
+P = 128
+ROWS = DIM // P
+HALF = 512
+QUART = 256
+EST = 128
+COUNT = DIM * L
+BN = (7, 3)
+TWICE = (2, 1)
+RING = 3
+KEEP = 1
+
+
+def tile_prgselfatt_pa_kernel(tc, x, attn_out, w_out, b_out, out):
+    nc = tc.nc
+    x_v = x.rearrange("n (p j) t h w -> n p j (t h w)", j=ROWS)
+    o_v = out.rearrange("n (p j) t h w -> n p j (t h w)", j=ROWS)
+    a_v = attn_out.rearrange("n (p j) t h w -> n p j (t h w)", j=4)
+    w_v = w_out.rearrange("(p j) k -> p (j k)", j=ROWS)
+    b_v = b_out.rearrange("(p j) -> p j", j=ROWS)
+
+    with ExitStack() as ctx:
+        sb = ctx.enter_context(tc.tile_pool(name="sb", bufs=1))
+        ps = ctx.enter_context(tc.psum_pool(name="ps", bufs=1))
+        ctx.enter_context(tc.manual_schedule())
+
+        def tile(name, shape, dtype):
+            return sb.tile(shape, dtype, name=name, align_bytes=64)
+
+        def per_sample(name, shape, dtype):
+            return [tile("%s%d" % (name, n), shape, dtype) for n in range(SAMPLES)]
+
+        a_raw = {}
+        w_raw = {}
+
+        def load_a(n, h0, h1):
+            t = tile("a%d%d" % (n, h0), [P, 4, (h1 - h0) * HALF], BF16)
+            nc.sync.dma_start(out=t[:], in_=a_v[n, :, :, h0 * HALF : h1 * HALF])
+            for qi in range(2 * h0, 2 * h1):
+                a_raw[n, qi] = t[:, :, (qi - 2 * h0) * QUART : (qi - 2 * h0 + 1) * QUART]
+
+        def load_w(g0, g1):
+            t = tile("w%d" % g0, [P, (g1 - g0) * 2 * INNER], BF16)
+            nc.sync.dma_start(out=t[:], in_=w_v[:, g0 * 2 * INNER : g1 * 2 * INNER])
+            for g in range(g0, g1):
+                w_raw[g] = t[:, (g - g0) * 2 * INNER : (g - g0 + 1) * 2 * INNER]
+
+        b_bf = tile("b_bf", [P, ROWS], BF16)
+        nc.scalar.dma_start(out=b_bf[:], in_=b_v)
+        load_w(0, 1)
+        load_a(0, 0, 1)
+        load_w(1, 2)
+        load_w(2, 4)
+        load_a(0, 1, 2)
+        load_a(1, 0, 2)
+        x_sb = per_sample("x", [P, ROWS, L], BF16)
+        for n in range(SAMPLES):
+            nc.sync.dma_start(out=x_sb[n][:], in_=x_v[n])
+
+        ident = tile("ident", [P, P], F32)
+        make_identity(nc, ident[:])
+        avg = tile("avg", [P, P], F32)
+        nc.gpsimd.memset(avg[:], 1.0 / COUNT)
+        neg_half = tile("neg_half", [P, 1], F32)
+        nc.gpsimd.memset(neg_half[:], -0.5)
+
+        w_codes = tile("w_codes", [P, DIM], U32)
+        w_scales = tile("w_scales", [P, DIM], U8)
+        a_codes = per_sample("a_codes", [P, L], U32)
+        a_scales = per_sample("a_scales", [P, L], U8)
+        a_grouped = per_sample("a_grouped", [P, L, 4], BF16)
+        w_grouped = tile("w_grouped", [P, DIM * 4], BF16)
+        o_sb = per_sample("o", [P, ROWS, L], F32)
+        small = ps.tile([P, HALF], F32, name="small")
+
+        squared = [2 * ROWS - BN[n] for n in range(SAMPLES)]
+        folds = [(BN[n] + 1) // 2 for n in range(SAMPLES)]
+        lead = [squared[n] + folds[n] + 1 for n in range(SAMPLES)]
+        slots = [lead[n] + 2 * BN[n] for n in range(SAMPLES)]
+        b32 = tile("b32", [P, ROWS], F32)
+        est = per_sample("est", [P, 1], F32)
+        neg_s = per_sample("neg_s", [P, 1], F32)
+        bs = per_sample("bs", [P, ROWS], F32)
+        parts = [tile("parts%d" % n, [P, slots[n], 3], F32) for n in range(SAMPLES)]
+        bs16 = per_sample("bs16", [P, ROWS], F32)
+        dev = per_sample("dev", [P, ROWS, 4], F32)
+        scr_v = per_sample("scr_v", [P, 32], F32)
+        scr_s = per_sample("scr_s", [P, 32], F32)
+        scr_q = per_sample("scr_q", [P, 32], F32)
+        delta = per_sample("delta", [P, 1], F32)
+        nd = per_sample("nd", [P, 1], F32)
+        ve = per_sample("ve", [P, 1], F32)
+        rstd = per_sample("rstd", [P, 1], F32)
+        cc = per_sample("cc", [P, ROWS], F32)
+
+        for n in range(SAMPLES):
+            k = lead[n] - 1
+            nc.scalar.activation(out=parts[n][:, k, 2:3], in_=neg_half[:], func=ACT.Copy, scale=-2.0 * EPS * COUNT / P)
+        for n in range(SAMPLES):
+            k = lead[n] - 1
+            nc.scalar.activation(out=scr_s[n][:, 0:ROWS], in_=b_bf[:], func=ACT.Copy, scale=float(L // (HALF // 2)),
+                                 accum_out=parts[n][:, k, 1:2])
+        nc.scalar.activation(out=b32[:], in_=b_bf[:], func=ACT.Copy)
+
+        free = {"s": [0, 1, 2], "v": [0, 1, 2]}
+        where = {}
+        held = {}
+        sums = {}
+
+        def bank(ring, key):
+            i = free[ring].pop(0)
+            where[key] = (ring, i)
+            held[key] = ps.tile([P, HALF], F32, name="bank", tag="%s%d" % (ring, i))
+            return held[key]
+
+        def release(key):
+            ring, i = where.pop(key)
+            held.pop(key)
+            free[ring].append(i)
+
+        def junk():
+            return sb.tile([P, HALF], F32, name="junk", tag="junk", bufs=2, align_bytes=64)
+
+        def interleave(n, qi, eng="v"):
+            src = a_raw[n, qi].rearrange("p t (c i) -> p c t i", i=4)
+            dst = a_grouped[n][:, qi * QUART : (qi + 1) * QUART, :].rearrange("p (c i) t -> p c t i", i=4)
+            if eng == "v":
+                nc.vector.tensor_copy(out=dst, in_=src)
+            else:
+                nc.scalar.copy(out=dst, in_=src)
+
+        def quant_a(n, qi, count=1):
+            cols = slice(qi * QUART, (qi + count) * QUART)
+            nc.vector.quantize_mx(
+                out=a_codes[n][:, cols].bitcast(E4M3),
+                scales=a_scales[n][:, cols],
+                in_=a_grouped[n][:, cols, :].rearrange("p c t -> p (c t)"),
+            )
+
+        def transpose_w(g, ring="v"):
+            words = w_raw[g].bitcast(F32)
+            t = bank(ring, ("w", g))
+            for jj in range(2):
+                base = jj * (INNER // 2)
+                for u in range(2):
+                    c0 = (2 * jj + u) * P
+                    nc.tensor.transpose(t[:, c0 : c0 + P], words[:, base + u : base + INNER // 2 : 2], ident[:])
+
+        def copy_w(g):
+            t = held["w", g]
+            dst = w_grouped[:, g * 1024 : (g + 1) * 1024].bitcast(F32).rearrange("p (j r u) -> p j r u", j=2, u=2)
+            nc.scalar.copy(out=dst, in_=t[:].rearrange("p (j u r) -> p j r u", j=2, u=2))
+            release(("w", g))
+
+        def quant_w(g, count=1):
+            cols = slice(g * 2 * P, (g + count) * 2 * P)
+            nc.vector.quantize_mx(
+                out=w_codes[:, cols].bitcast(E5M2),
+                scales=w_scales[:, cols],
+                in_=w_grouped[:, g * 1024 : (g + count) * 1024],
+            )
+
+        def product(dst, n, j, h, start=True, stop=True, width=HALF):
+            m = slice(j * P, (j + 1) * P)
+            cols = slice(h * HALF, h * HALF + width)
+            nc.tensor.matmul_mx(
+                out=dst[:, 0:width],
+                lhsT=w_codes[:, m].bitcast(E5M2),
+                lhsT_scale=w_scales[:, m],
+                rhs=a_codes[n][:, cols].bitcast(E4M3),
+                rhs_scale=a_scales[n][:, cols],
+                start=start,
+                stop=stop,
+            )
+
+        all_tiles = [(j, h) for j in range(ROWS) for h in range(2)]
+        v_tiles = [all_tiles[2 * ROWS - BN[n] :] for n in range(SAMPLES)]
+        v_rows = [sorted(set(j for j, h in v_tiles[n])) for n in range(SAMPLES)]
+        s_tiles = [[(j, h) for h in range(2) for j in range(ROWS) if (j, h) not in v_tiles[n]] for n in range(SAMPLES)]
+        kept = [(0, j, h) for j, h in v_tiles[0][BN[0] - KEEP :]]
+
+        def mm(n, jh, ring):
+            product(bank(ring, (n, jh)), n, jh[0], jh[1])
+
+        nxt = {"s0": 0, "s1": 0, "v0": 0, "v1": 0, "m0": 0, "m1": 0, "q0": 0, "q1": 0, "b0": 0, "b1": 0, "r0": 0, "r1": 0, "f0": 0, "f1": 0}
+
+        def step(key):
+            nxt[key] = nxt[key] + 1
+            return nxt[key] - 1
+
+        def v_mm(n):
+            mm(n, v_tiles[n][step("v%d" % n)], "v")
+
+        def s_mm(n):
+            mm(n, s_tiles[n][step("s%d" % n)], "s")
+
+        def s_sum(n):
+            i = step("m%d" % n) + TWICE[n]
+            if i == TWICE[n]:
+                sums[n] = ps.tile([P, HALF], F32, name="sums", tag="sums")
+            j, h = s_tiles[n][i]
+            product(sums[n], n, j, h, start=(i == TWICE[n]), stop=(i == squared[n] - 1))
+
+        def square(n):
+            i = step("q%d" % n)
+            jh = s_tiles[n][i]
+            nc.scalar.activation(out=junk()[:], in_=held[n, jh][:], func=ACT.Square,
+                                 bias=bs[n][:, jh[0] : jh[0] + 1], accum_out=parts[n][:, i, 2:3])
+            release((n, jh))
+
+        def row_sum(n):
+            i = step("r%d" % n)
+            nc.scalar.activation(out=junk()[:], in_=held[n, s_tiles[n][i]][:], func=ACT.Copy, scale=2.0 / HALF,
+                                 accum_out=parts[n][:, lead[n] - 2 - TWICE[n] + i, 1:2])
+
+        def est_mm(n, ring="s"):
+            product(bank(ring, ("e", n)), n, 0, 0, width=EST)
+
+        def estimate(n):
+            nc.scalar.activation(out=junk()[:, 0:EST], in_=held["e", n][:, 0:EST], func=ACT.Identity,
+                                 bias=b32[:, 0:1], accum_out=est[n][:])
+            release(("e", n))
+
+        def across(n, c0, src):
+            w = src.shape[1]
+            dst = small[:, n * 128 + c0 : n * 128 + c0 + w]
+            nc.tensor.matmul(out=dst, lhsT=avg[:], rhs=src, start=True, stop=True)
+            return dst
+
+        def shift_mm(n):
+            held["s", n] = across(n, 0, est[n][:])
+
+        def shift_a(n):
+            nc.scalar.activation(out=neg_s[n][:], in_=held["s", n], func=ACT.Copy, scale=-float(COUNT // (P * EST)))
+
+        def shift_b(n):
+            nc.scalar.activation(out=bs[n][:], in_=b32[:], func=ACT.Identity, bias=neg_s[n][:])
+
+        def v_stat(n):
+            i = step("b%d" % n)
+            j, h = v_tiles[n][i]
+            k = lead[n] + 2 * i
+            nc.vector.bn_stats(out=parts[n][:, k : k + 2, :].rearrange("p a b -> p (a b)"), in_=held[n, (j, h)][:])
+            if (n, j, h) not in kept:
+                release((n, (j, h)))
+
+        def fold_a(n):
+            nc.scalar.activation(out=bs16[n][:], in_=bs[n][:], func=ACT.Copy, scale=16.0)
+
+        def fold_b(n, r0, r1):
+            for r in range(r0, r1):
+                j = v_rows[n][r]
+                mine = [i for i in range(BN[n]) if v_tiles[n][i][0] == j]
+                means = parts[n][:, lead[n] + 2 * mine[0] : lead[n] + 2 * mine[-1] + 2, 1]
+                nc.scalar.activation(out=dev[n][:, r, 0 : 2 * len(mine)], in_=means, func=ACT.Square, scale=16.0,
+                                     bias=bs16[n][:, j : j + 1], accum_out=parts[n][:, squared[n] + r, 2:3])
+
+        def sum_read(n, eng="s"):
+            if eng == "s":
+                nc.scalar.activation(out=junk()[:], in_=sums[n][:], func=ACT.Copy, scale=2.0 / HALF,
+                                     accum_out=parts[n][:, lead[n] - 2, 1:2])
+            else:
+                t = sb.tile([P, HALF], F32, name="junk_v", align_bytes=64)
+                nc.vector.tensor_scalar(out=t[:], in0=sums[n][:], scalar1=2.0 / HALF, scalar2=None, op0=ALU.mult,
+                                        op1=ALU.add, accum_out=parts[n][:, lead[n] - 2, 1:2])
+
+        def mean_mm(n):
+            held["d", n] = across(n, 16, parts[n][:, lead[n] - 2 - TWICE[n] :, 1])
+
+        def mean_a(n):
+            w = slots[n] - lead[n] + 2 + TWICE[n]
+            nc.vector.tensor_scalar(out=scr_v[n][:, 0:w], in0=held["d", n], scalar1=float(HALF // 2), scalar2=neg_s[n][:],
+                                    op0=ALU.mult, op1=ALU.add, accum_out=delta[n][:])
+
+        def mean_b(n):
+            nc.vector.tensor_scalar(out=nd[n][:], in0=delta[n][:], scalar1=delta[n][:], scalar2=-1.0 / slots[n],
+                                    op0=ALU.mult, op1=ALU.mult)
+
+        def var_mm(n):
+            held["q", n] = across(n, 64, parts[n][:, :, 2])
+
+        def var_read(n):
+            nc.scalar.activation(out=scr_q[n][:, 0 : slots[n]], in_=held["q", n], func=ACT.Identity, bias=nd[n][:],
+                                 accum_out=ve[n][:])
+
+        def scale_and_offsets(n):
+            nc.gpsimd.tensor_tensor(out=rstd[n][:], in0=ve[n][:], in1=neg_half[:], op=ALU.pow)
+            nc.gpsimd.tensor_scalar(out=cc[n][:], in0=bs[n][:], scalar1=delta[n][:], scalar2=rstd[n][:],
+                                    op0=ALU.subtract, op1=ALU.mult)
+
+        def x_pre(n, j, eng, c0=0, c1=L):
+            if eng == "g":
+                nc.gpsimd.tensor_scalar(out=o_sb[n][:, j, c0:c1], in0=x_sb[n][:, j, c0:c1], scalar1=1.0,
+                                        scalar2=cc[n][:, j : j + 1], op0=ALU.mult, op1=ALU.add)
+            else:
+                nc.scalar.activation(out=o_sb[n][:, j, c0:c1], in_=x_sb[n][:, j, c0:c1], func=ACT.Identity,
+                                     bias=cc[n][:, j : j + 1])
+
+        def finish(n, j, h):
+            dst = o_sb[n][:, j, h * HALF : (h + 1) * HALF]
+            nc.vector.scalar_tensor_tensor(out=dst, in0=held[n, (j, h)][:], scalar=rstd[n][:], in1=dst,
+                                           op0=ALU.mult, op1=ALU.add)
+            release((n, (j, h)))
+
+        def store(n, j0, j1, c0=0, c1=L):
+            nc.sync.dma_start(out=o_v[n, :, j0:j1, c0:c1], in_=o_sb[n][:, j0:j1, c0:c1])
+
+        f_rows = [ROWS - 1 - r for r in range(ROWS)]
+        f_tiles = [(j, h) for j in f_rows for h in (1, 0)]
+        todo = [(n, j, h) for n in range(SAMPLES) for j, h in f_tiles if (n, j, h) not in kept]
+
+        def f_mm():
+            if todo:
+                n, j, h = todo.pop(0)
+                mm(n, (j, h), "v")
+
+        def fin(n):
+            j, h = f_tiles[step("f%d" % n)]
+            finish(n, j, h)
+
+        def st(n, upto, count):
+            tiles = f_tiles[upto - count : upto]
+            if count == 1:
+                j, h = tiles[0]
+                store(n, j, j + 1, h * HALF, (h + 1) * HALF)
+            else:
+                store(n, tiles[-1][0], tiles[0][0] + 1)
+
+        transpose_w(0)
+        transpose_w(1)
+        copy_w(0)
+        interleave(0, 1, "s")
+        copy_w(1)
+        interleave(0, 0)
+        quant_w(0)
+        quant_a(0, 0)
+        quant_a(0, 1)
+        quant_w(1)
+        interleave(0, 2)
+        est_mm(0)
+        transpose_w(2)
+        estimate(0)
+        copy_w(2)
+        quant_w(2)
+        interleave(0, 3)
+        shift_mm(0)
+        transpose_w(3)
+        s_mm(0)
+        s_mm(0)
+        s_mm(0)
+        s_sum(0)
+        s_sum(0)
+        shift_a(0)
+        copy_w(3)
+        shift_b(0)
+        row_sum(0)
+        square(0)
+        row_sum(0)
+        square(0)
+        fold_a(0)
+        square(0)
+        quant_w(3)
+        quant_a(0, 2, 2)
+        interleave(1, 0)
+        interleave(1, 1)
+        s_mm(0)
+        s_sum(0)
+        v_mm(0)
+        v_mm(0)
+        s_mm(0)
+        s_sum(0)
+        v_mm(0)
+        s_mm(0)
+        s_sum(0)
+        square(0)
+        square(0)
+        v_stat(0)
+        quant_a(1, 0, 2)
+        v_stat(0)
+        v_stat(0)
+        est_mm(1)
+        s_sum(0)
+        v_mm(0)
+        s_sum(0)
+        s_mm(0)
+        v_mm(0)
+        v_mm(0)
+        estimate(1)
+        square(0)
+        sum_read(0)
+        v_stat(0)
+        v_stat(0)
+        v_stat(0)
+        shift_mm(1)
+        s_mm(0)
+        v_mm(0)
+        s_mm(0)
+        s_sum(1)
+        shift_a(1)
+        square(0)
+        shift_b(1)
+        square(0)
+        fold_b(0, 0, 3)
+        square(0)
+        v_stat(0)
+        interleave(1, 2)
+        interleave(1, 3)
+        s_mm(1)
+        s_sum(1)
+        s_sum(1)
+        mean_mm(0)
+        s_mm(1)
+        s_sum(1)
+        s_mm(1)
+        fold_b(0, 3, 4)
+        row_sum(1)
+        square(1)
+        mean_a(0)
+        quant_a(1, 2, 2)
+        mean_b(0)
+        var_mm(0)
+        s_sum(1)
+        s_sum(1)
+        v_mm(1)
+        v_mm(1)
+        s_mm(1)
+        s_sum(1)
+        var_read(0)
+        fold_a(1)
+        square(1)
+        square(1)
+        v_stat(1)
+        v_stat(1)
+        scale_and_offsets(0)
+        x_pre(0, f_rows[1], "g")
+        x_pre(0, f_rows[2], "g")
+        x_pre(0, f_rows[3], "g")
+        x_pre(0, f_rows[4], "g")
+        x_pre(0, f_rows[5], "g")
+        v_mm(1)
+        s_mm(1)
+        s_sum(1)
+        f_mm()
+        s_mm(1)
+        s_sum(1)
+        x_pre(0, f_rows[0], "s", HALF, L)
+        x_pre(0, f_rows[0], "s", 0, HALF)
+        square(1)
+        square(1)
+        square(1)
+        v_stat(1)
+        fin(0)
+        fin(0)
+        st(0, 1, 1)
+        st(0, 2, 1)
+        f_mm()
+        s_mm(1)
+        s_sum(1)
+        f_mm()
+        s_mm(1)
+        s_sum(1)
+        f_mm()
+        s_mm(1)
+        s_sum(1)
+        fold_b(1, 0, 2)
+        square(1)
+        square(1)
+        sum_read(1)
+        square(1)
+        fin(0)
+        fin(0)
+        fin(0)
+        st(0, 4, 2)
+        f_mm()
+        s_mm(1)
+        f_mm()
+        s_mm(1)
+        f_mm()
+        s_mm(1)
+        mean_mm(1)
+        square(1)
+        square(1)
+        square(1)
+        fin(0)
+        fin(0)
+        fin(0)
+        st(0, 6, 2)
+        st(0, 8, 2)
+        f_mm()
+        s_mm(1)
+        f_mm()
+        f_mm()
+        square(1)
+        x_pre(0, f_rows[6], "s")
+        fin(0)
+        mean_a(1)
+        fin(0)
+        mean_b(1)
+        fin(0)
+        st(0, 10, 2)
+        var_mm(1)
+        f_mm()
+        f_mm()
+        f_mm()
+        var_read(1)
+        x_pre(0, f_rows[7], "s")
+        fin(0)
+        fin(0)
+        fin(0)
+        scale_and_offsets(1)
+        x_pre(1, f_rows[1], "g")
+        x_pre(1, f_rows[4], "g")
+        x_pre(1, f_rows[7], "g")
+        st(0, 12, 2)
+        st(0, 14, 2)
+        f_mm()
+        f_mm()
+        f_mm()
+        x_pre(1, f_rows[0], "s", HALF, L)
+        x_pre(1, f_rows[0], "s", 0, HALF)
+        x_pre(1, f_rows[2], "s")
+        x_pre(1, f_rows[3], "s")
+        x_pre(1, f_rows[5], "s")
+        x_pre(1, f_rows[6], "s")
+        fin(0)
+        fin(0)
+        fin(1)
+        st(0, 16, 2)
+        f_mm()
+        f_mm()
+        f_mm()
+        fin(1)
+        fin(1)
+        fin(1)
+        st(1, 2, 2)
+        st(1, 4, 2)
+        f_mm()
+        f_mm()
+        f_mm()
+        fin(1)
+        fin(1)
+        fin(1)
+        st(1, 6, 2)
+        f_mm()
+        f_mm()
+        f_mm()
+        fin(1)
+        fin(1)
+        fin(1)
+        st(1, 8, 2)
+        st(1, 10, 2)
+        f_mm()
+        f_mm()
+        f_mm()
+        fin(1)
+        fin(1)
+        fin(1)
+        st(1, 12, 2)
+        f_mm()
+        f_mm()
+        f_mm()
+        fin(1)
+        fin(1)
+        fin(1)
+        st(1, 14, 2)
+        st(1, 16, 2)

@@ -22,10 +22,10 @@ HALF = 512
 QUART = 256
 EST = 128
 COUNT = DIM * L
-BN = (7, 3)
-TWICE = (2, 1)
+BN = (8, 4)
+TWICE = (2, 0)
 RING = 3
-KEEP = 1
+KEEP = 2
 
 
 def tile_prgselfatt_pa_kernel(tc, x, attn_out, w_out, b_out, out):
@@ -39,7 +39,8 @@ def tile_prgselfatt_pa_kernel(tc, x, attn_out, w_out, b_out, out):
     with ExitStack() as ctx:
         sb = ctx.enter_context(tc.tile_pool(name="sb", bufs=1))
         ps = ctx.enter_context(tc.psum_pool(name="ps", bufs=1))
-        ctx.enter_context(tc.manual_schedule())
+        eng = mybir.EngineType
+        ctx.enter_context(tc.manual_schedule(engines={eng.Activation, eng.DVE, eng.Pool, eng.SP}))
 
         def tile(name, shape, dtype):
             return sb.tile(shape, dtype, name=name, align_bytes=64)
@@ -85,29 +86,38 @@ def tile_prgselfatt_pa_kernel(tc, x, attn_out, w_out, b_out, out):
         w_scales = tile("w_scales", [P, DIM], U8)
         a_codes = per_sample("a_codes", [P, L], U32)
         a_scales = per_sample("a_scales", [P, L], U8)
-        a_grouped = per_sample("a_grouped", [P, L, 4], BF16)
+        halves = [tile("staged_first", [P, HALF, 4], BF16), tile("staged_late", [P, HALF, 4], BF16)]
+        staged = {(0, qi): halves[qi // 2][:, (qi % 2) * QUART : (qi % 2 + 1) * QUART, :] for qi in range(4)}
         w_grouped = tile("w_grouped", [P, DIM * 4], BF16)
         o_sb = per_sample("o", [P, ROWS, L], F32)
         small = ps.tile([P, HALF], F32, name="small")
 
+        all_tiles = [(j, h) for j in range(ROWS) for h in range(2)]
+        v_set = [all_tiles[2 * ROWS - BN[n] :] for n in range(SAMPLES)]
+        v_tiles = [sorted(v_set[0][:-2], key=lambda jh: jh[1]) + v_set[0][-2:], sorted(v_set[1], key=lambda jh: jh[1])]
+        v_rows = [sorted(set(j for j, h in v_tiles[n])) for n in range(SAMPLES)]
         squared = [2 * ROWS - BN[n] for n in range(SAMPLES)]
-        folds = [(BN[n] + 1) // 2 for n in range(SAMPLES)]
+        folds = [len(v_rows[n]) for n in range(SAMPLES)]
         lead = [squared[n] + folds[n] + 1 for n in range(SAMPLES)]
         slots = [lead[n] + 2 * BN[n] for n in range(SAMPLES)]
         b32 = tile("b32", [P, ROWS], F32)
-        est = per_sample("est", [P, 1], F32)
-        neg_s = per_sample("neg_s", [P, 1], F32)
-        bs = per_sample("bs", [P, ROWS], F32)
+        shift = per_sample("shift", [P, 1], F32)
+        nb = per_sample("nb", [P, ROWS], F32)
         parts = [tile("parts%d" % n, [P, slots[n], 3], F32) for n in range(SAMPLES)]
-        bs16 = per_sample("bs16", [P, ROWS], F32)
+        first = [lead[n] - 2 - TWICE[n] for n in range(SAMPLES)]
+        est = per_sample("est", [P, 1], F32)
+        nb16 = per_sample("nb16", [P, ROWS], F32)
         dev = per_sample("dev", [P, ROWS, 4], F32)
         scr_v = per_sample("scr_v", [P, 32], F32)
         scr_s = per_sample("scr_s", [P, 32], F32)
         scr_q = per_sample("scr_q", [P, 32], F32)
         delta = per_sample("delta", [P, 1], F32)
+        share = per_sample("share", [P, 1], F32)
         nd = per_sample("nd", [P, 1], F32)
         ve = per_sample("ve", [P, 1], F32)
         rstd = per_sample("rstd", [P, 1], F32)
+        bd = per_sample("bd", [P, ROWS], F32)
+        cc_g = per_sample("cc_g", [P, ROWS], F32)
         cc = per_sample("cc", [P, ROWS], F32)
 
         for n in range(SAMPLES):
@@ -139,8 +149,15 @@ def tile_prgselfatt_pa_kernel(tc, x, attn_out, w_out, b_out, out):
             return sb.tile([P, HALF], F32, name="junk", tag="junk", bufs=2, align_bytes=64)
 
         def interleave(n, qi, eng="v"):
-            src = a_raw[n, qi].rearrange("p t (c i) -> p c t i", i=4)
-            dst = a_grouped[n][:, qi * QUART : (qi + 1) * QUART, :].rearrange("p (c i) t -> p c t i", i=4)
+            if n == 1:
+                staged[n, qi] = sb.tile([P, QUART, 4], BF16, name="staged_late", align_bytes=64)[:]
+            dst = staged[n, qi]
+            src = a_raw[n, qi]
+            if eng == "g":
+                nc.gpsimd.tensor_copy(out=dst, in_=src.rearrange("p t c -> p c t"))
+                return
+            dst = dst.rearrange("p (c i) t -> p c t i", i=4)
+            src = src.rearrange("p t (c i) -> p c t i", i=4)
             if eng == "v":
                 nc.vector.tensor_copy(out=dst, in_=src)
             else:
@@ -148,10 +165,11 @@ def tile_prgselfatt_pa_kernel(tc, x, attn_out, w_out, b_out, out):
 
         def quant_a(n, qi, count=1):
             cols = slice(qi * QUART, (qi + count) * QUART)
+            src = staged[n, qi] if count == 1 else halves[qi // 2][:]
             nc.vector.quantize_mx(
                 out=a_codes[n][:, cols].bitcast(E4M3),
                 scales=a_scales[n][:, cols],
-                in_=a_grouped[n][:, cols, :].rearrange("p c t -> p (c t)"),
+                in_=src.rearrange("p c t -> p (c t)"),
             )
 
         def transpose_w(g, ring="v"):
@@ -190,11 +208,9 @@ def tile_prgselfatt_pa_kernel(tc, x, attn_out, w_out, b_out, out):
                 stop=stop,
             )
 
-        all_tiles = [(j, h) for j in range(ROWS) for h in range(2)]
-        v_tiles = [all_tiles[2 * ROWS - BN[n] :] for n in range(SAMPLES)]
-        v_rows = [sorted(set(j for j, h in v_tiles[n])) for n in range(SAMPLES)]
         s_tiles = [[(j, h) for h in range(2) for j in range(ROWS) if (j, h) not in v_tiles[n]] for n in range(SAMPLES)]
-        kept = [(0, j, h) for j, h in v_tiles[0][BN[0] - KEEP :]]
+        s_tiles[1] = [jh for jh in s_tiles[1] if jh[0] != 0] + [(0, 0), (0, 1)]
+        kept = [(0, ROWS - 1, 0), (0, ROWS - 1, 1), (1, 0, 0), (1, 0, 1)]
 
         def mm(n, jh, ring):
             product(bank(ring, (n, jh)), n, jh[0], jh[1])
@@ -221,22 +237,23 @@ def tile_prgselfatt_pa_kernel(tc, x, attn_out, w_out, b_out, out):
         def square(n):
             i = step("q%d" % n)
             jh = s_tiles[n][i]
-            nc.scalar.activation(out=junk()[:], in_=held[n, jh][:], func=ACT.Square,
-                                 bias=bs[n][:, jh[0] : jh[0] + 1], accum_out=parts[n][:, i, 2:3])
-            release((n, jh))
+            nc.scalar.activation(out=junk()[:], in_=held[n, jh][:], func=ACT.Square, scale=-1.0,
+                                 bias=nb[n][:, jh[0] : jh[0] + 1], accum_out=parts[n][:, i, 2:3])
+            if (n, jh[0], jh[1]) not in kept:
+                release((n, jh))
 
         def row_sum(n):
             i = step("r%d" % n)
             nc.scalar.activation(out=junk()[:], in_=held[n, s_tiles[n][i]][:], func=ACT.Copy, scale=2.0 / HALF,
                                  accum_out=parts[n][:, lead[n] - 2 - TWICE[n] + i, 1:2])
 
-        def est_mm(n, ring="s"):
-            product(bank(ring, ("e", n)), n, 0, 0, width=EST)
+        def est_mm(n):
+            held["e", n] = small[:, 256 + n * EST : 256 + (n + 1) * EST]
+            product(held["e", n], n, 0, 0, width=EST)
 
         def estimate(n):
             nc.scalar.activation(out=junk()[:, 0:EST], in_=held["e", n][:, 0:EST], func=ACT.Identity,
                                  bias=b32[:, 0:1], accum_out=est[n][:])
-            release(("e", n))
 
         def across(n, c0, src):
             w = src.shape[1]
@@ -248,29 +265,29 @@ def tile_prgselfatt_pa_kernel(tc, x, attn_out, w_out, b_out, out):
             held["s", n] = across(n, 0, est[n][:])
 
         def shift_a(n):
-            nc.scalar.activation(out=neg_s[n][:], in_=held["s", n], func=ACT.Copy, scale=-float(COUNT // (P * EST)))
+            nc.scalar.activation(out=shift[n][:], in_=held["s", n], func=ACT.Copy, scale=float(COUNT // (P * EST)))
 
         def shift_b(n):
-            nc.scalar.activation(out=bs[n][:], in_=b32[:], func=ACT.Identity, bias=neg_s[n][:])
+            nc.scalar.activation(out=nb[n][:], in_=b32[:], func=ACT.Identity, scale=-1.0, bias=shift[n][:])
 
         def v_stat(n):
             i = step("b%d" % n)
             j, h = v_tiles[n][i]
-            k = lead[n] + 2 * i
+            k = lead[n] + 2 * v_set[n].index((j, h))
             nc.vector.bn_stats(out=parts[n][:, k : k + 2, :].rearrange("p a b -> p (a b)"), in_=held[n, (j, h)][:])
             if (n, j, h) not in kept:
                 release((n, (j, h)))
 
         def fold_a(n):
-            nc.scalar.activation(out=bs16[n][:], in_=bs[n][:], func=ACT.Copy, scale=16.0)
+            nc.scalar.activation(out=nb16[n][:], in_=nb[n][:], func=ACT.Copy, scale=16.0)
 
         def fold_b(n, r0, r1):
             for r in range(r0, r1):
                 j = v_rows[n][r]
-                mine = [i for i in range(BN[n]) if v_tiles[n][i][0] == j]
+                mine = [i for i in range(BN[n]) if v_set[n][i][0] == j]
                 means = parts[n][:, lead[n] + 2 * mine[0] : lead[n] + 2 * mine[-1] + 2, 1]
-                nc.scalar.activation(out=dev[n][:, r, 0 : 2 * len(mine)], in_=means, func=ACT.Square, scale=16.0,
-                                     bias=bs16[n][:, j : j + 1], accum_out=parts[n][:, squared[n] + r, 2:3])
+                nc.scalar.activation(out=dev[n][:, r, 0 : 2 * len(mine)], in_=means, func=ACT.Square, scale=-16.0,
+                                     bias=nb16[n][:, j : j + 1], accum_out=parts[n][:, squared[n] + r, 2:3])
 
         def sum_read(n, eng="s"):
             if eng == "s":
@@ -282,16 +299,18 @@ def tile_prgselfatt_pa_kernel(tc, x, attn_out, w_out, b_out, out):
                                         op1=ALU.add, accum_out=parts[n][:, lead[n] - 2, 1:2])
 
         def mean_mm(n):
-            held["d", n] = across(n, 16, parts[n][:, lead[n] - 2 - TWICE[n] :, 1])
+            held["d", n] = across(n, 16, parts[n][:, first[n] :, 1])
 
         def mean_a(n):
             w = slots[n] - lead[n] + 2 + TWICE[n]
-            nc.vector.tensor_scalar(out=scr_v[n][:, 0:w], in0=held["d", n], scalar1=float(HALF // 2), scalar2=neg_s[n][:],
+            nc.vector.tensor_scalar(out=scr_v[n][:, 0:w], in0=held["d", n], scalar1=-float(HALF // 2), scalar2=shift[n][:],
                                     op0=ALU.mult, op1=ALU.add, accum_out=delta[n][:])
 
         def mean_b(n):
-            nc.vector.tensor_scalar(out=nd[n][:], in0=delta[n][:], scalar1=delta[n][:], scalar2=-1.0 / slots[n],
-                                    op0=ALU.mult, op1=ALU.mult)
+            nc.scalar.activation(out=share[n][:], in_=delta[n][:], func=ACT.Copy, scale=-1.0 / slots[n])
+
+        def mean_c(n):
+            nc.scalar.activation(out=nd[n][:], in_=share[n][:], func=ACT.Copy, scale=delta[n][:])
 
         def var_mm(n):
             held["q", n] = across(n, 64, parts[n][:, :, 2])
@@ -300,21 +319,29 @@ def tile_prgselfatt_pa_kernel(tc, x, attn_out, w_out, b_out, out):
             nc.scalar.activation(out=scr_q[n][:, 0 : slots[n]], in_=held["q", n], func=ACT.Identity, bias=nd[n][:],
                                  accum_out=ve[n][:])
 
-        def scale_and_offsets(n):
+        def centre(n):
+            nc.scalar.activation(out=bd[n][:], in_=nb[n][:], func=ACT.Identity, scale=-1.0, bias=delta[n][:])
+
+        def inv_std(n):
             nc.gpsimd.tensor_tensor(out=rstd[n][:], in0=ve[n][:], in1=neg_half[:], op=ALU.pow)
-            nc.gpsimd.tensor_scalar(out=cc[n][:], in0=bs[n][:], scalar1=delta[n][:], scalar2=rstd[n][:],
-                                    op0=ALU.subtract, op1=ALU.mult)
+
+        def offsets(n):
+            nc.scalar.activation(out=cc[n][:], in_=bd[n][:], func=ACT.Copy, scale=rstd[n][:])
 
         def x_pre(n, j, eng, c0=0, c1=L):
             if eng == "g":
                 nc.gpsimd.tensor_scalar(out=o_sb[n][:, j, c0:c1], in0=x_sb[n][:, j, c0:c1], scalar1=1.0,
-                                        scalar2=cc[n][:, j : j + 1], op0=ALU.mult, op1=ALU.add)
+                                        scalar2=cc_g[n][:, j : j + 1], op0=ALU.mult, op1=ALU.add)
             else:
                 nc.scalar.activation(out=o_sb[n][:, j, c0:c1], in_=x_sb[n][:, j, c0:c1], func=ACT.Identity,
                                      bias=cc[n][:, j : j + 1])
 
         def finish(n, j, h):
             dst = o_sb[n][:, j, h * HALF : (h + 1) * HALF]
+            if (n, j, h) in kept:
+                nc.vector.scalar_tensor_tensor(out=dst, in0=dst, scalar=rstd[n][:],
+                                               in1=x_sb[n][:, j, h * HALF : (h + 1) * HALF], op0=ALU.mult, op1=ALU.add)
+                return
             nc.vector.scalar_tensor_tensor(out=dst, in0=held[n, (j, h)][:], scalar=rstd[n][:], in1=dst,
                                            op0=ALU.mult, op1=ALU.add)
             release((n, (j, h)))
@@ -322,9 +349,22 @@ def tile_prgselfatt_pa_kernel(tc, x, attn_out, w_out, b_out, out):
         def store(n, j0, j1, c0=0, c1=L):
             nc.sync.dma_start(out=o_v[n, :, j0:j1, c0:c1], in_=o_sb[n][:, j0:j1, c0:c1])
 
-        f_rows = [ROWS - 1 - r for r in range(ROWS)]
-        f_tiles = [(j, h) for j in f_rows for h in (1, 0)]
-        todo = [(n, j, h) for n in range(SAMPLES) for j, h in f_tiles if (n, j, h) not in kept]
+        f_rows = [[ROWS - 1 - r for r in range(ROWS)], list(range(ROWS))]
+        f_tiles = [[(j, h) for j in f_rows[n] for h in range(2)] for n in range(SAMPLES)]
+        todo = [(n, j, h) for n in range(SAMPLES) for j, h in f_tiles[n] if (n, j, h) not in kept]
+
+        def park(n, h):
+            j = f_rows[n][0]
+            dst = o_sb[n][:, j, h * HALF : (h + 1) * HALF]
+            if n == 0:
+                nc.vector.tensor_scalar(out=dst, in0=held[n, (j, h)][:], scalar1=nb[n][:, j : j + 1], scalar2=delta[n][:],
+                                        op0=ALU.subtract, op1=ALU.add)
+            else:
+                nc.scalar.activation(out=dst, in_=held[n, (j, h)][:], func=ACT.Identity, bias=bd[n][:, j : j + 1])
+            release((n, (j, h)))
+
+        def offsets_g(n):
+            nc.vector.tensor_scalar(out=cc_g[n][:], in0=bd[n][:], scalar1=rstd[n][:], scalar2=None, op0=ALU.mult)
 
         def f_mm():
             if todo:
@@ -332,252 +372,162 @@ def tile_prgselfatt_pa_kernel(tc, x, attn_out, w_out, b_out, out):
                 mm(n, (j, h), "v")
 
         def fin(n):
-            j, h = f_tiles[step("f%d" % n)]
+            j, h = f_tiles[n][step("f%d" % n)]
             finish(n, j, h)
 
         def st(n, upto, count):
-            tiles = f_tiles[upto - count : upto]
+            tiles = f_tiles[n][upto - count : upto]
             if count == 1:
                 j, h = tiles[0]
                 store(n, j, j + 1, h * HALF, (h + 1) * HALF)
             else:
-                store(n, tiles[-1][0], tiles[0][0] + 1)
+                store(n, min(tiles)[0], max(tiles)[0] + 1)
 
         transpose_w(0)
-        transpose_w(1)
         copy_w(0)
-        interleave(0, 1, "s")
-        copy_w(1)
         interleave(0, 0)
+        interleave(0, 1, "s")
         quant_w(0)
         quant_a(0, 0)
+        transpose_w(1)
+        est_mm(0)
+        copy_w(1)
+        estimate(0)
         quant_a(0, 1)
         quant_w(1)
-        interleave(0, 2)
-        est_mm(0)
         transpose_w(2)
-        estimate(0)
-        copy_w(2)
-        quant_w(2)
-        interleave(0, 3)
         shift_mm(0)
         transpose_w(3)
-        s_mm(0)
-        s_mm(0)
-        s_mm(0)
-        s_sum(0)
-        s_sum(0)
+        copy_w(2)
         shift_a(0)
         copy_w(3)
         shift_b(0)
-        row_sum(0)
-        square(0)
-        row_sum(0)
-        square(0)
-        fold_a(0)
-        square(0)
+        interleave(0, 2)
+        quant_w(2)
+        interleave(0, 3)
         quant_w(3)
         quant_a(0, 2, 2)
-        interleave(1, 0)
-        interleave(1, 1)
-        s_mm(0)
-        s_sum(0)
-        v_mm(0)
-        v_mm(0)
-        s_mm(0)
-        s_sum(0)
-        v_mm(0)
-        s_mm(0)
-        s_sum(0)
-        square(0)
-        square(0)
-        v_stat(0)
-        quant_a(1, 0, 2)
-        v_stat(0)
-        v_stat(0)
-        est_mm(1)
-        s_sum(0)
-        v_mm(0)
-        s_sum(0)
-        s_mm(0)
-        v_mm(0)
-        v_mm(0)
-        estimate(1)
-        square(0)
+        interleave(1, 0, "g")
+
+        def s_tile(n):
+            s_mm(n)
+            if nxt["r%d" % n] < TWICE[n]:
+                row_sum(n)
+            square(n)
+
+        def v_tile(n):
+            v_mm(n)
+            v_stat(n)
+
+        def sum_passes(n, count):
+            for r in range(min(count, squared[n] - TWICE[n] - nxt["m%d" % n])):
+                s_sum(n)
+
+        def f_tile(n):
+            i = nxt["f%d" % n]
+            j, h = f_tiles[n][i]
+            if (n, j, h) not in kept:
+                f_mm()
+            fin(n)
+            if n == 0 and i < 2:
+                st(n, i + 1, 1)
+            elif i % 2 == 1:
+                st(n, i + 1, 2)
+
+        for i in range(BN[0]):
+            if i < squared[0] - 2:
+                s_tile(0)
+            v_tile(0)
+            sum_passes(0, 1)
+            if i == 0:
+                fold_a(0)
+            if i == 2:
+                quant_a(1, 0)
+                interleave(1, 1, "g")
+                est_mm(1)
+            if i == 4:
+                estimate(1)
+                shift_mm(1)
+            if i == 4:
+                quant_a(1, 1)
+                interleave(1, 2, "g")
+        sum_passes(0, 99)
         sum_read(0)
-        v_stat(0)
-        v_stat(0)
-        v_stat(0)
-        shift_mm(1)
-        s_mm(0)
-        v_mm(0)
-        s_mm(0)
-        s_sum(1)
         shift_a(1)
-        square(0)
+        s_tile(0)
         shift_b(1)
-        square(0)
-        fold_b(0, 0, 3)
-        square(0)
-        v_stat(0)
-        interleave(1, 2)
-        interleave(1, 3)
-        s_mm(1)
-        s_sum(1)
-        s_sum(1)
         mean_mm(0)
-        s_mm(1)
-        s_sum(1)
-        s_mm(1)
-        fold_b(0, 3, 4)
-        row_sum(1)
-        square(1)
+        quant_a(1, 2)
+        interleave(1, 3, "g")
+        v_tile(1)
         mean_a(0)
-        quant_a(1, 2, 2)
-        mean_b(0)
+
+        park(0, 0)
+        park(0, 1)
+        quant_a(1, 3)
+        fold_b(0, 0, folds[0])
+        s_tile(0)
         var_mm(0)
-        s_sum(1)
-        s_sum(1)
-        v_mm(1)
-        v_mm(1)
-        s_mm(1)
-        s_sum(1)
-        var_read(0)
+        mean_b(0)
+        centre(0)
+        s_tile(1)
         fold_a(1)
-        square(1)
-        square(1)
-        v_stat(1)
-        v_stat(1)
-        scale_and_offsets(0)
-        x_pre(0, f_rows[1], "g")
-        x_pre(0, f_rows[2], "g")
-        x_pre(0, f_rows[3], "g")
-        x_pre(0, f_rows[4], "g")
-        x_pre(0, f_rows[5], "g")
-        v_mm(1)
-        s_mm(1)
-        s_sum(1)
-        f_mm()
-        s_mm(1)
-        s_sum(1)
-        x_pre(0, f_rows[0], "s", HALF, L)
-        x_pre(0, f_rows[0], "s", 0, HALF)
-        square(1)
-        square(1)
-        square(1)
-        v_stat(1)
-        fin(0)
-        fin(0)
-        st(0, 1, 1)
-        st(0, 2, 1)
-        f_mm()
-        s_mm(1)
-        s_sum(1)
-        f_mm()
-        s_mm(1)
-        s_sum(1)
-        f_mm()
-        s_mm(1)
-        s_sum(1)
-        fold_b(1, 0, 2)
-        square(1)
-        square(1)
+        mean_c(0)
+        var_read(0)
+        inv_std(0)
+        sum_passes(1, 4)
+        for i in range(1):
+            v_tile(1)
+        for i in range(2):
+            s_tile(1)
+        offsets(0)
+        f_tile(0)
+        f_tile(0)
+        offsets_g(0)
+        x_pre(0, f_rows[0][1], "s", 0, HALF)
+        x_pre(0, f_rows[0][1], "s", HALF, L)
+        for r in range(2, ROWS):
+            x_pre(0, f_rows[0][r], "g")
+        f_tile(0)
+        s_tile(1)
+        f_tile(0)
+        while nxt["b1"] < BN[1]:
+            v_tile(1)
+            s_tile(1)
+            f_tile(0)
+            sum_passes(1, 2)
+        while nxt["q1"] < squared[1] - 5:
+            f_tile(0)
+            s_tile(1)
+            sum_passes(1, 2)
+        sum_passes(1, 99)
         sum_read(1)
-        square(1)
-        fin(0)
-        fin(0)
-        fin(0)
-        st(0, 4, 2)
-        f_mm()
-        s_mm(1)
-        f_mm()
-        s_mm(1)
-        f_mm()
-        s_mm(1)
         mean_mm(1)
-        square(1)
-        square(1)
-        square(1)
-        fin(0)
-        fin(0)
-        fin(0)
-        st(0, 6, 2)
-        st(0, 8, 2)
-        f_mm()
-        s_mm(1)
-        f_mm()
-        f_mm()
-        square(1)
-        x_pre(0, f_rows[6], "s")
-        fin(0)
+        s_tile(1)
+        fold_b(1, 0, folds[1])
+        for i in range(2):
+            f_tile(0)
         mean_a(1)
-        fin(0)
+        while nxt["q1"] < squared[1] - 1:
+            s_tile(1)
         mean_b(1)
-        fin(0)
-        st(0, 10, 2)
+        centre(1)
+        s_tile(1)
         var_mm(1)
-        f_mm()
-        f_mm()
-        f_mm()
+        mean_c(1)
+        park(1, 0)
         var_read(1)
-        x_pre(0, f_rows[7], "s")
-        fin(0)
-        fin(0)
-        fin(0)
-        scale_and_offsets(1)
-        x_pre(1, f_rows[1], "g")
-        x_pre(1, f_rows[4], "g")
-        x_pre(1, f_rows[7], "g")
-        st(0, 12, 2)
-        st(0, 14, 2)
-        f_mm()
-        f_mm()
-        f_mm()
-        x_pre(1, f_rows[0], "s", HALF, L)
-        x_pre(1, f_rows[0], "s", 0, HALF)
-        x_pre(1, f_rows[2], "s")
-        x_pre(1, f_rows[3], "s")
-        x_pre(1, f_rows[5], "s")
-        x_pre(1, f_rows[6], "s")
-        fin(0)
-        fin(0)
-        fin(1)
-        st(0, 16, 2)
-        f_mm()
-        f_mm()
-        f_mm()
-        fin(1)
-        fin(1)
-        fin(1)
-        st(1, 2, 2)
-        st(1, 4, 2)
-        f_mm()
-        f_mm()
-        f_mm()
-        fin(1)
-        fin(1)
-        fin(1)
-        st(1, 6, 2)
-        f_mm()
-        f_mm()
-        f_mm()
-        fin(1)
-        fin(1)
-        fin(1)
-        st(1, 8, 2)
-        st(1, 10, 2)
-        f_mm()
-        f_mm()
-        f_mm()
-        fin(1)
-        fin(1)
-        fin(1)
-        st(1, 12, 2)
-        f_mm()
-        f_mm()
-        f_mm()
-        fin(1)
-        fin(1)
-        fin(1)
-        st(1, 14, 2)
-        st(1, 16, 2)
+        inv_std(1)
+        park(1, 1)
+        offsets(1)
+        while nxt["f0"] < 2 * ROWS:
+            f_tile(0)
+        f_tile(1)
+        f_tile(1)
+        offsets_g(1)
+        x_pre(1, f_rows[1][1], "s", 0, HALF)
+        x_pre(1, f_rows[1][1], "s", HALF, L)
+        for r in range(2, ROWS):
+            x_pre(1, f_rows[1][r], "g" if r % 2 == 1 else "s")
+        while nxt["f1"] < 2 * ROWS:
+            f_tile(1)

from contextlib import ExitStack

import concourse.mybir as mybir
from concourse.masks import make_identity

F32 = mybir.dt.float32
BF16 = mybir.dt.bfloat16
U32 = mybir.dt.uint32
U8 = mybir.dt.uint8
E4M3 = mybir.dt.float8_e4m3fn_x4
E5M2 = mybir.dt.float8_e5m2_x4
ALU = mybir.AluOpType
ACT = mybir.ActivationFunctionType

SAMPLES, DIM, INNER, L = 2, 1024, 512, 1024
EPS = 1e-5
FLOPS = 2 * SAMPLES * DIM * INNER * L

P = 128
ROWS = DIM // P
HALF = 512
QUART = 256
EST = 128
COUNT = DIM * L
BN = (8, 4)
TWICE = (2, 0)
RING = 3
KEEP = 2


def tile_prgselfatt_pa_kernel(tc, x, attn_out, w_out, b_out, out):
    nc = tc.nc
    x_v = x.rearrange("n (p j) t h w -> n p j (t h w)", j=ROWS)
    o_v = out.rearrange("n (p j) t h w -> n p j (t h w)", j=ROWS)
    a_v = attn_out.rearrange("n (p j) t h w -> n p j (t h w)", j=4)
    w_v = w_out.rearrange("(p j) k -> p (j k)", j=ROWS)
    b_v = b_out.rearrange("(p j) -> p j", j=ROWS)

    with ExitStack() as ctx:
        sb = ctx.enter_context(tc.tile_pool(name="sb", bufs=1))
        ps = ctx.enter_context(tc.psum_pool(name="ps", bufs=1))
        eng = mybir.EngineType
        ctx.enter_context(tc.manual_schedule(engines={eng.Activation, eng.DVE, eng.Pool, eng.SP}))

        def tile(name, shape, dtype):
            return sb.tile(shape, dtype, name=name, align_bytes=64)

        def per_sample(name, shape, dtype):
            return [tile("%s%d" % (name, n), shape, dtype) for n in range(SAMPLES)]

        a_raw = {}
        w_raw = {}

        def load_a(n, h0, h1):
            t = tile("a%d%d" % (n, h0), [P, 4, (h1 - h0) * HALF], BF16)
            nc.sync.dma_start(out=t[:], in_=a_v[n, :, :, h0 * HALF : h1 * HALF])
            for qi in range(2 * h0, 2 * h1):
                a_raw[n, qi] = t[:, :, (qi - 2 * h0) * QUART : (qi - 2 * h0 + 1) * QUART]

        def load_w(g0, g1):
            t = tile("w%d" % g0, [P, (g1 - g0) * 2 * INNER], BF16)
            nc.sync.dma_start(out=t[:], in_=w_v[:, g0 * 2 * INNER : g1 * 2 * INNER])
            for g in range(g0, g1):
                w_raw[g] = t[:, (g - g0) * 2 * INNER : (g - g0 + 1) * 2 * INNER]

        b_bf = tile("b_bf", [P, ROWS], BF16)
        nc.scalar.dma_start(out=b_bf[:], in_=b_v)
        load_w(0, 1)
        load_a(0, 0, 1)
        load_w(1, 2)
        load_w(2, 4)
        load_a(0, 1, 2)
        load_a(1, 0, 2)
        x_sb = per_sample("x", [P, ROWS, L], BF16)
        for n in range(SAMPLES):
            nc.sync.dma_start(out=x_sb[n][:], in_=x_v[n])

        ident = tile("ident", [P, P], F32)
        make_identity(nc, ident[:])
        avg = tile("avg", [P, P], F32)
        nc.gpsimd.memset(avg[:], 1.0 / COUNT)
        neg_half = tile("neg_half", [P, 1], F32)
        nc.gpsimd.memset(neg_half[:], -0.5)

        w_codes = tile("w_codes", [P, DIM], U32)
        w_scales = tile("w_scales", [P, DIM], U8)
        a_codes = per_sample("a_codes", [P, L], U32)
        a_scales = per_sample("a_scales", [P, L], U8)
        halves = [tile("staged_first", [P, HALF, 4], BF16), tile("staged_late", [P, HALF, 4], BF16)]
        staged = {(0, qi): halves[qi // 2][:, (qi % 2) * QUART : (qi % 2 + 1) * QUART, :] for qi in range(4)}
        w_grouped = tile("w_grouped", [P, DIM * 4], BF16)
        o_sb = per_sample("o", [P, ROWS, L], F32)
        small = ps.tile([P, HALF], F32, name="small")

        all_tiles = [(j, h) for j in range(ROWS) for h in range(2)]
        v_set = [all_tiles[2 * ROWS - BN[n] :] for n in range(SAMPLES)]
        v_tiles = [sorted(v_set[0][:-2], key=lambda jh: jh[1]) + v_set[0][-2:], sorted(v_set[1], key=lambda jh: jh[1])]
        v_rows = [sorted(set(j for j, h in v_tiles[n])) for n in range(SAMPLES)]
        squared = [2 * ROWS - BN[n] for n in range(SAMPLES)]
        folds = [len(v_rows[n]) for n in range(SAMPLES)]
        lead = [squared[n] + folds[n] + 1 for n in range(SAMPLES)]
        slots = [lead[n] + 2 * BN[n] for n in range(SAMPLES)]
        b32 = tile("b32", [P, ROWS], F32)
        shift = per_sample("shift", [P, 1], F32)
        nb = per_sample("nb", [P, ROWS], F32)
        parts = [tile("parts%d" % n, [P, slots[n], 3], F32) for n in range(SAMPLES)]
        first = [lead[n] - 2 - TWICE[n] for n in range(SAMPLES)]
        est = per_sample("est", [P, 1], F32)
        nb16 = per_sample("nb16", [P, ROWS], F32)
        dev = per_sample("dev", [P, ROWS, 4], F32)
        scr_v = per_sample("scr_v", [P, 32], F32)
        scr_s = per_sample("scr_s", [P, 32], F32)
        scr_q = per_sample("scr_q", [P, 32], F32)
        delta = per_sample("delta", [P, 1], F32)
        share = per_sample("share", [P, 1], F32)
        nd = per_sample("nd", [P, 1], F32)
        ve = per_sample("ve", [P, 1], F32)
        rstd = per_sample("rstd", [P, 1], F32)
        bd = per_sample("bd", [P, ROWS], F32)
        cc_g = per_sample("cc_g", [P, ROWS], F32)
        cc = per_sample("cc", [P, ROWS], F32)

        for n in range(SAMPLES):
            k = lead[n] - 1
            nc.scalar.activation(out=parts[n][:, k, 2:3], in_=neg_half[:], func=ACT.Copy, scale=-2.0 * EPS * COUNT / P)
        for n in range(SAMPLES):
            k = lead[n] - 1
            nc.scalar.activation(out=scr_s[n][:, 0:ROWS], in_=b_bf[:], func=ACT.Copy, scale=float(L // (HALF // 2)),
                                 accum_out=parts[n][:, k, 1:2])
        nc.scalar.activation(out=b32[:], in_=b_bf[:], func=ACT.Copy)

        free = {"s": [0, 1, 2], "v": [0, 1, 2]}
        where = {}
        held = {}
        sums = {}

        def bank(ring, key):
            i = free[ring].pop(0)
            where[key] = (ring, i)
            held[key] = ps.tile([P, HALF], F32, name="bank", tag="%s%d" % (ring, i))
            return held[key]

        def release(key):
            ring, i = where.pop(key)
            held.pop(key)
            free[ring].append(i)

        def junk():
            return sb.tile([P, HALF], F32, name="junk", tag="junk", bufs=2, align_bytes=64)

        def interleave(n, qi, eng="v"):
            if n == 1:
                staged[n, qi] = sb.tile([P, QUART, 4], BF16, name="staged_late", align_bytes=64)[:]
            dst = staged[n, qi]
            src = a_raw[n, qi]
            if eng == "g":
                nc.gpsimd.tensor_copy(out=dst, in_=src.rearrange("p t c -> p c t"))
                return
            dst = dst.rearrange("p (c i) t -> p c t i", i=4)
            src = src.rearrange("p t (c i) -> p c t i", i=4)
            if eng == "v":
                nc.vector.tensor_copy(out=dst, in_=src)
            else:
                nc.scalar.copy(out=dst, in_=src)

        def quant_a(n, qi, count=1):
            cols = slice(qi * QUART, (qi + count) * QUART)
            src = staged[n, qi] if count == 1 else halves[qi // 2][:]
            nc.vector.quantize_mx(
                out=a_codes[n][:, cols].bitcast(E4M3),
                scales=a_scales[n][:, cols],
                in_=src.rearrange("p c t -> p (c t)"),
            )

        def transpose_w(g, ring="v"):
            words = w_raw[g].bitcast(F32)
            t = bank(ring, ("w", g))
            for jj in range(2):
                base = jj * (INNER // 2)
                for u in range(2):
                    c0 = (2 * jj + u) * P
                    nc.tensor.transpose(t[:, c0 : c0 + P], words[:, base + u : base + INNER // 2 : 2], ident[:])

        def copy_w(g):
            t = held["w", g]
            dst = w_grouped[:, g * 1024 : (g + 1) * 1024].bitcast(F32).rearrange("p (j r u) -> p j r u", j=2, u=2)
            nc.scalar.copy(out=dst, in_=t[:].rearrange("p (j u r) -> p j r u", j=2, u=2))
            release(("w", g))

        def quant_w(g, count=1):
            cols = slice(g * 2 * P, (g + count) * 2 * P)
            nc.vector.quantize_mx(
                out=w_codes[:, cols].bitcast(E5M2),
                scales=w_scales[:, cols],
                in_=w_grouped[:, g * 1024 : (g + count) * 1024],
            )

        def product(dst, n, j, h, start=True, stop=True, width=HALF):
            m = slice(j * P, (j + 1) * P)
            cols = slice(h * HALF, h * HALF + width)
            nc.tensor.matmul_mx(
                out=dst[:, 0:width],
                lhsT=w_codes[:, m].bitcast(E5M2),
                lhsT_scale=w_scales[:, m],
                rhs=a_codes[n][:, cols].bitcast(E4M3),
                rhs_scale=a_scales[n][:, cols],
                start=start,
                stop=stop,
            )

        s_tiles = [[(j, h) for h in range(2) for j in range(ROWS) if (j, h) not in v_tiles[n]] for n in range(SAMPLES)]
        s_tiles[1] = [jh for jh in s_tiles[1] if jh[0] != 0] + [(0, 0), (0, 1)]
        kept = [(0, ROWS - 1, 0), (0, ROWS - 1, 1), (1, 0, 0), (1, 0, 1)]

        def mm(n, jh, ring):
            product(bank(ring, (n, jh)), n, jh[0], jh[1])

        nxt = {"s0": 0, "s1": 0, "v0": 0, "v1": 0, "m0": 0, "m1": 0, "q0": 0, "q1": 0, "b0": 0, "b1": 0, "r0": 0, "r1": 0, "f0": 0, "f1": 0}

        def step(key):
            nxt[key] = nxt[key] + 1
            return nxt[key] - 1

        def v_mm(n):
            mm(n, v_tiles[n][step("v%d" % n)], "v")

        def s_mm(n):
            mm(n, s_tiles[n][step("s%d" % n)], "s")

        def s_sum(n):
            i = step("m%d" % n) + TWICE[n]
            if i == TWICE[n]:
                sums[n] = ps.tile([P, HALF], F32, name="sums", tag="sums")
            j, h = s_tiles[n][i]
            product(sums[n], n, j, h, start=(i == TWICE[n]), stop=(i == squared[n] - 1))

        def square(n):
            i = step("q%d" % n)
            jh = s_tiles[n][i]
            nc.scalar.activation(out=junk()[:], in_=held[n, jh][:], func=ACT.Square, scale=-1.0,
                                 bias=nb[n][:, jh[0] : jh[0] + 1], accum_out=parts[n][:, i, 2:3])
            if (n, jh[0], jh[1]) not in kept:
                release((n, jh))

        def row_sum(n):
            i = step("r%d" % n)
            nc.scalar.activation(out=junk()[:], in_=held[n, s_tiles[n][i]][:], func=ACT.Copy, scale=2.0 / HALF,
                                 accum_out=parts[n][:, lead[n] - 2 - TWICE[n] + i, 1:2])

        def est_mm(n):
            held["e", n] = small[:, 256 + n * EST : 256 + (n + 1) * EST]
            product(held["e", n], n, 0, 0, width=EST)

        def estimate(n):
            nc.scalar.activation(out=junk()[:, 0:EST], in_=held["e", n][:, 0:EST], func=ACT.Identity,
                                 bias=b32[:, 0:1], accum_out=est[n][:])

        def across(n, c0, src):
            w = src.shape[1]
            dst = small[:, n * 128 + c0 : n * 128 + c0 + w]
            nc.tensor.matmul(out=dst, lhsT=avg[:], rhs=src, start=True, stop=True)
            return dst

        def shift_mm(n):
            held["s", n] = across(n, 0, est[n][:])

        def shift_a(n):
            nc.scalar.activation(out=shift[n][:], in_=held["s", n], func=ACT.Copy, scale=float(COUNT // (P * EST)))

        def shift_b(n):
            nc.scalar.activation(out=nb[n][:], in_=b32[:], func=ACT.Identity, scale=-1.0, bias=shift[n][:])

        def v_stat(n):
            i = step("b%d" % n)
            j, h = v_tiles[n][i]
            k = lead[n] + 2 * v_set[n].index((j, h))
            nc.vector.bn_stats(out=parts[n][:, k : k + 2, :].rearrange("p a b -> p (a b)"), in_=held[n, (j, h)][:])
            if (n, j, h) not in kept:
                release((n, (j, h)))

        def fold_a(n):
            nc.scalar.activation(out=nb16[n][:], in_=nb[n][:], func=ACT.Copy, scale=16.0)

        def fold_b(n, r0, r1):
            for r in range(r0, r1):
                j = v_rows[n][r]
                mine = [i for i in range(BN[n]) if v_set[n][i][0] == j]
                means = parts[n][:, lead[n] + 2 * mine[0] : lead[n] + 2 * mine[-1] + 2, 1]
                nc.scalar.activation(out=dev[n][:, r, 0 : 2 * len(mine)], in_=means, func=ACT.Square, scale=-16.0,
                                     bias=nb16[n][:, j : j + 1], accum_out=parts[n][:, squared[n] + r, 2:3])

        def sum_read(n, eng="s"):
            if eng == "s":
                nc.scalar.activation(out=junk()[:], in_=sums[n][:], func=ACT.Copy, scale=2.0 / HALF,
                                     accum_out=parts[n][:, lead[n] - 2, 1:2])
            else:
                t = sb.tile([P, HALF], F32, name="junk_v", align_bytes=64)
                nc.vector.tensor_scalar(out=t[:], in0=sums[n][:], scalar1=2.0 / HALF, scalar2=None, op0=ALU.mult,
                                        op1=ALU.add, accum_out=parts[n][:, lead[n] - 2, 1:2])

        def mean_mm(n):
            held["d", n] = across(n, 16, parts[n][:, first[n] :, 1])

        def mean_a(n):
            w = slots[n] - lead[n] + 2 + TWICE[n]
            nc.vector.tensor_scalar(out=scr_v[n][:, 0:w], in0=held["d", n], scalar1=-float(HALF // 2), scalar2=shift[n][:],
                                    op0=ALU.mult, op1=ALU.add, accum_out=delta[n][:])

        def mean_b(n):
            nc.scalar.activation(out=share[n][:], in_=delta[n][:], func=ACT.Copy, scale=-1.0 / slots[n])

        def mean_c(n):
            nc.scalar.activation(out=nd[n][:], in_=share[n][:], func=ACT.Copy, scale=delta[n][:])

        def var_mm(n):
            held["q", n] = across(n, 64, parts[n][:, :, 2])

        def var_read(n):
            nc.scalar.activation(out=scr_q[n][:, 0 : slots[n]], in_=held["q", n], func=ACT.Identity, bias=nd[n][:],
                                 accum_out=ve[n][:])

        def centre(n):
            nc.scalar.activation(out=bd[n][:], in_=nb[n][:], func=ACT.Identity, scale=-1.0, bias=delta[n][:])

        def inv_std(n):
            nc.gpsimd.tensor_tensor(out=rstd[n][:], in0=ve[n][:], in1=neg_half[:], op=ALU.pow)

        def offsets(n):
            nc.scalar.activation(out=cc[n][:], in_=bd[n][:], func=ACT.Copy, scale=rstd[n][:])

        def x_pre(n, j, eng, c0=0, c1=L):
            if eng == "g":
                nc.gpsimd.tensor_scalar(out=o_sb[n][:, j, c0:c1], in0=x_sb[n][:, j, c0:c1], scalar1=1.0,
                                        scalar2=cc_g[n][:, j : j + 1], op0=ALU.mult, op1=ALU.add)
            else:
                nc.scalar.activation(out=o_sb[n][:, j, c0:c1], in_=x_sb[n][:, j, c0:c1], func=ACT.Identity,
                                     bias=cc[n][:, j : j + 1])

        def finish(n, j, h):
            dst = o_sb[n][:, j, h * HALF : (h + 1) * HALF]
            if (n, j, h) in kept:
                nc.vector.scalar_tensor_tensor(out=dst, in0=dst, scalar=rstd[n][:],
                                               in1=x_sb[n][:, j, h * HALF : (h + 1) * HALF], op0=ALU.mult, op1=ALU.add)
                return
            nc.vector.scalar_tensor_tensor(out=dst, in0=held[n, (j, h)][:], scalar=rstd[n][:], in1=dst,
                                           op0=ALU.mult, op1=ALU.add)
            release((n, (j, h)))

        def store(n, j0, j1, c0=0, c1=L):
            nc.sync.dma_start(out=o_v[n, :, j0:j1, c0:c1], in_=o_sb[n][:, j0:j1, c0:c1])

        f_rows = [[ROWS - 1 - r for r in range(ROWS)], list(range(ROWS))]
        f_tiles = [[(j, h) for j in f_rows[n] for h in range(2)] for n in range(SAMPLES)]
        todo = [(n, j, h) for n in range(SAMPLES) for j, h in f_tiles[n] if (n, j, h) not in kept]

        def park(n, h):
            j = f_rows[n][0]
            dst = o_sb[n][:, j, h * HALF : (h + 1) * HALF]
            if n == 0:
                nc.vector.tensor_scalar(out=dst, in0=held[n, (j, h)][:], scalar1=nb[n][:, j : j + 1], scalar2=delta[n][:],
                                        op0=ALU.subtract, op1=ALU.add)
            else:
                nc.scalar.activation(out=dst, in_=held[n, (j, h)][:], func=ACT.Identity, bias=bd[n][:, j : j + 1])
            release((n, (j, h)))

        def offsets_g(n):
            nc.vector.tensor_scalar(out=cc_g[n][:], in0=bd[n][:], scalar1=rstd[n][:], scalar2=None, op0=ALU.mult)

        def f_mm():
            if todo:
                n, j, h = todo.pop(0)
                mm(n, (j, h), "v")

        def fin(n):
            j, h = f_tiles[n][step("f%d" % n)]
            finish(n, j, h)

        def st(n, upto, count):
            tiles = f_tiles[n][upto - count : upto]
            if count == 1:
                j, h = tiles[0]
                store(n, j, j + 1, h * HALF, (h + 1) * HALF)
            else:
                store(n, min(tiles)[0], max(tiles)[0] + 1)

        transpose_w(0)
        copy_w(0)
        interleave(0, 0)
        interleave(0, 1, "s")
        quant_w(0)
        quant_a(0, 0)
        transpose_w(1)
        est_mm(0)
        copy_w(1)
        estimate(0)
        quant_a(0, 1)
        quant_w(1)
        transpose_w(2)
        shift_mm(0)
        transpose_w(3)
        copy_w(2)
        shift_a(0)
        copy_w(3)
        shift_b(0)
        interleave(0, 2)
        quant_w(2)
        interleave(0, 3)
        quant_w(3)
        quant_a(0, 2, 2)
        interleave(1, 0, "g")

        def s_tile(n):
            s_mm(n)
            if nxt["r%d" % n] < TWICE[n]:
                row_sum(n)
            square(n)

        def v_tile(n):
            v_mm(n)
            v_stat(n)

        def sum_passes(n, count):
            for r in range(min(count, squared[n] - TWICE[n] - nxt["m%d" % n])):
                s_sum(n)

        def f_tile(n):
            i = nxt["f%d" % n]
            j, h = f_tiles[n][i]
            if (n, j, h) not in kept:
                f_mm()
            fin(n)
            if n == 0 and i < 2:
                st(n, i + 1, 1)
            elif i % 2 == 1:
                st(n, i + 1, 2)

        for i in range(BN[0]):
            if i < squared[0] - 2:
                s_tile(0)
            v_tile(0)
            sum_passes(0, 1)
            if i == 0:
                fold_a(0)
            if i == 2:
                quant_a(1, 0)
                interleave(1, 1, "g")
                est_mm(1)
            if i == 4:
                estimate(1)
                shift_mm(1)
            if i == 4:
                quant_a(1, 1)
                interleave(1, 2, "g")
        sum_passes(0, 99)
        sum_read(0)
        shift_a(1)
        s_tile(0)
        shift_b(1)
        mean_mm(0)
        quant_a(1, 2)
        interleave(1, 3, "g")
        v_tile(1)
        mean_a(0)

        park(0, 0)
        park(0, 1)
        quant_a(1, 3)
        fold_b(0, 0, folds[0])
        s_tile(0)
        var_mm(0)
        mean_b(0)
        centre(0)
        s_tile(1)
        fold_a(1)
        mean_c(0)
        var_read(0)
        inv_std(0)
        sum_passes(1, 4)
        for i in range(1):
            v_tile(1)
        for i in range(2):
            s_tile(1)
        offsets(0)
        f_tile(0)
        f_tile(0)
        offsets_g(0)
        x_pre(0, f_rows[0][1], "s", 0, HALF)
        x_pre(0, f_rows[0][1], "s", HALF, L)
        for r in range(2, ROWS):
            x_pre(0, f_rows[0][r], "g")
        f_tile(0)
        s_tile(1)
        f_tile(0)
        while nxt["b1"] < BN[1]:
            v_tile(1)
            s_tile(1)
            f_tile(0)
            sum_passes(1, 2)
        while nxt["q1"] < squared[1] - 5:
            f_tile(0)
            s_tile(1)
            sum_passes(1, 2)
        sum_passes(1, 99)
        sum_read(1)
        mean_mm(1)
        s_tile(1)
        fold_b(1, 0, folds[1])
        for i in range(2):
            f_tile(0)
        mean_a(1)
        while nxt["q1"] < squared[1] - 1:
            s_tile(1)
        mean_b(1)
        centre(1)
        s_tile(1)
        var_mm(1)
        mean_c(1)
        park(1, 0)
        var_read(1)
        inv_std(1)
        park(1, 1)
        offsets(1)
        while nxt["f0"] < 2 * ROWS:
            f_tile(0)
        f_tile(1)
        f_tile(1)
        offsets_g(1)
        x_pre(1, f_rows[1][1], "s", 0, HALF)
        x_pre(1, f_rows[1][1], "s", HALF, L)
        for r in range(2, ROWS):
            x_pre(1, f_rows[1][r], "g" if r % 2 == 1 else "s")
        while nxt["f1"] < 2 * ROWS:
            f_tile(1)
